import numpy as np
import ml_dtypes


def mxq(x, axis, fmt="e4m3"):
    dtype, down = {"e4m3": (ml_dtypes.float8_e4m3fn, 7), "e5m2": (ml_dtypes.float8_e5m2, 14)}[fmt]
    v = np.moveaxis(np.asarray(x, np.float32).astype(ml_dtypes.bfloat16).astype(np.float64), axis, -1)
    blocks = v.reshape(v.shape[:-1] + (-1, 32))
    amax = np.abs(blocks).max(-1, keepdims=True)
    byte = np.maximum(np.where(amax > 0, np.frexp(amax)[1] - 1 + 127, 0) - down, 1)
    scale = np.exp2(byte - 127.0)
    codes = (blocks / scale).astype(np.float32).astype(dtype).astype(np.float64)
    return np.moveaxis((codes * scale).reshape(v.shape), -1, axis)


WIDE = False


def mx_kscale(k):
    if not WIDE:
        return np.ones(k)
    levels = np.array([10, -10, 5, -5, 0])
    a = np.random.permutation(np.resize(levels, k // 512 * 4)).reshape(k // 512, 4)
    idx = np.arange(k)
    return np.exp2(a[idx // 512, idx % 128 // 32])


BF16 = ml_dtypes.bfloat16


def bf(x):
    return np.asarray(x, np.float32).astype(BF16)


def f64(x):
    return np.asarray(x).astype(np.float64)


B, L, D, F = 128, 8, 512, 1024
EPS = 1e-12


def l2norm(w, axis):
    n = np.sqrt(np.sum(w * w, axis=axis, keepdims=True))
    return w / np.maximum(n, EPS)


def silu(z):
    return z / (1.0 + np.exp(-z))


def draw_w(k, n, s):
    a = np.random.standard_normal((L, k, n)) / s[:, None]
    return a / np.sqrt(np.sum(a * a, axis=1, keepdims=True)) * np.exp2(np.random.randint(-1, 2, (L, 1, n)))


def draw_gain():
    return np.random.choice([-1.0, 1.0], (1, F)) * (1.0 + 0.1 * np.random.standard_normal((1, F)))


def setup_inputs():
    s, t = mx_kscale(D), mx_kscale(F)
    c = np.sqrt(np.mean(1.0 / s**2))
    return {'x': bf(np.random.standard_normal((B, L, D)) * s),
            'W_gate': bf(draw_w(D, F, s)),
            'W_up': bf(draw_w(D, F, s)),
            'W_down': bf(draw_w(F, D, t)),
            's_u': bf(draw_gain() * c * t),
            's_v': bf(draw_gain() * c * 1.5 / np.sqrt(D))}


def reference(x, W_gate, W_up, W_down, s_u, s_v):
    Wg = l2norm(f64(W_gate), 1)
    Wu = l2norm(f64(W_up), 1)
    Wd = l2norm(f64(W_down), 1)
    xq = mxq(f64(x), 2, 'e4m3').transpose(1, 0, 2)
    u = xq @ mxq(Wg, 1, 'e4m3')
    v = xq @ mxq(Wu, 1, 'e4m3')
    u_scale = np.abs(f64(s_u)) * 1.0
    v_scale = np.abs(f64(s_v)) * np.sqrt(D)
    h = silu(v_scale * v) * (u_scale * u)
    out = (mxq(h, 2, 'e4m3') @ mxq(Wd, 1, 'e4m3')).transpose(1, 0, 2)
    return l2norm(out, -1)

@@ -1,0 +1,359 @@
+import math
+from contextlib import ExitStack
+
+from concourse import mybir
+from concourse.masks import make_identity
+
+F32 = mybir.dt.float32
+BF16 = mybir.dt.bfloat16
+U32 = mybir.dt.uint32
+U8 = mybir.dt.uint8
+FP8X4 = mybir.dt.float8_e4m3fn_x4
+ACT = mybir.ActivationFunctionType
+ALU = mybir.AluOpType
+
+P = 128
+B, L, D, F = 128, 8, 512, 1024
+FLOPS = 2 * B * L * (D * F * 2 + F * D)
+EPS2 = 1e-24
+MANUAL = True
+BD_ENG = ['g','g','g','g']
+
+
+def tile_npertokenswishglu_kernel(tc, x, W_gate, W_up, W_down, s_u, s_v, out):
+    nc = tc.nc
+    with ExitStack() as ctx:
+        const = ctx.enter_context(tc.tile_pool(name="const", bufs=1))
+        wpool = ctx.enter_context(tc.tile_pool(name="wpool", bufs=9))
+        grp = ctx.enter_context(tc.tile_pool(name="grp", bufs=4))
+        code = ctx.enter_context(tc.tile_pool(name="code", bufs=2))
+        small = ctx.enter_context(tc.tile_pool(name="small", bufs=3))
+        work = ctx.enter_context(tc.tile_pool(name="work", bufs=2))
+        pt = ctx.enter_context(tc.psum_pool(name="pt", bufs=3))
+        pr = ctx.enter_context(tc.psum_pool(name="pr", bufs=2))
+        pm = ctx.enter_context(tc.psum_pool(name="pm", bufs=1))
+        if MANUAL:
+            ctx.enter_context(tc.manual_schedule())
+
+        ident = const.tile([P, P], F32)
+        make_identity(nc, ident[:])
+        mhalf = const.tile([P, 8], F32)
+        nc.vector.memset(mhalf[:], -0.5)
+        gz = const.tile([P, P], F32)
+        nc.vector.memset(gz[:], 0.0)
+        xs = const.tile([P, L, D], BF16)
+        xg = const.tile([P, L * B * 4], BF16, align_bytes=64)
+        xc = const.tile([P, L * B], U32, align_bytes=64)
+        xsc = const.tile([P, L * B], U8, align_bytes=64)
+        su = const.tile([P, 8], F32)
+        sv = const.tile([P, 8], F32)
+
+        wt = {}
+        nsq = {}
+        rr = {}
+        rbank = {}
+        rsb = {}
+        gt = {}
+        cod = {}
+        st = {}
+
+        def load(l, unit):
+            if unit == "d":
+                t = wpool.tile([P, 8, D], BF16, tag="W", name="wd")
+                nc.sync.dma_start(
+                    out=t[:].rearrange("p (g e) n -> p g (e n)", g=4),
+                    in_=W_down[l].rearrange("(g p e) n -> p g (e n)", g=4, p=P, e=2),
+                )
+            else:
+                W = W_gate if unit == "g" else W_up
+                t = wpool.tile([P, 4, F], BF16, tag="W", name="wg")
+                nc.sync.dma_start(
+                    out=t[:].rearrange("p (u e) n -> p u (e n)", u=2),
+                    in_=W[l].rearrange("(u p e) n -> p u (e n)", u=2, p=P, e=2),
+                )
+            wt[(l, unit)] = t
+
+        def load_x():
+            nc.sync.dma_start(out=xs[:], in_=x)
+            nc.sync.dma_start(out=gz[0:4, :], in_=s_u.bitcast(F32).rearrange("o (c w) -> (o c) w", c=4))
+            nc.sync.dma_start(out=gz[4:8, :], in_=s_v.bitcast(F32).rearrange("o (c w) -> (o c) w", c=4))
+
+        def prep_x():
+            xw = xs[:].bitcast(F32)
+            xgw = xg[:].bitcast(F32).rearrange("p (l b u) -> p l b u", l=L, b=B, u=2)
+            for lp in range(L // 2):
+                xt = pt.tile([P, 512], F32, tag="T", name="xt")
+                for i in range(2):
+                    for u in range(2):
+                        nc.tensor.transpose(
+                            xt[:, (2 * i + u) * P : (2 * i + u + 1) * P],
+                            xw[:, 2 * lp + i, u * P : (u + 1) * P],
+                            ident[:],
+                        )
+                nc.vector.tensor_copy(
+                    out=xgw[:, 2 * lp : 2 * lp + 2, :, :],
+                    in_=xt[:].rearrange("p (i u b) -> p i b u", i=2, u=2, b=B),
+                )
+            gp = pt.tile([P, 512], F32, tag="T", name="gp")
+            nc.tensor.transpose(gp[:, 0:P], gz[:], ident[:])
+            nc.scalar.activation(out=su[:], in_=gp[:, 0:4].bitcast(BF16), func=ACT.Abs)
+            nc.scalar.activation(out=sv[:], in_=gp[:, 4:8].bitcast(BF16), func=ACT.Abs, scale=math.sqrt(D))
+            nc.vector.quantize_mx(out=xc[:].bitcast(FP8X4), scales=xsc[:], in_=xg[:])
+
+        def a_item(l, k):
+            if k < 4:
+                unit, cb, hf = "d", k // 2, k % 2
+            elif k < 8:
+                unit, cb, hf = "g", k - 4, 0
+            else:
+                unit, cb, hf = "u", k - 8, 0
+            if k % 4 == 0:
+                shape = [P, 2, 4] if unit == "d" else [P, 1, 8]
+                nsq[(l, unit)] = small.tile(shape, F32, tag="nsq" + unit, name="nsq")
+            ww = wt[(l, unit)][:].bitcast(F32)
+            tp = pt.tile([P, 512], F32, tag="T", name="tp")
+            for j in range(4):
+                nc.tensor.transpose(tp[:, j * P : (j + 1) * P], ww[:, 4 * hf + j, cb * P : (cb + 1) * P], ident[:])
+            tv = tp[:].bitcast(BF16).rearrange("p (k e) -> p k e", e=2)
+            for e in range(2):
+                junk = work.tile([P, 512], BF16, tag="junk", name="junk")
+                nc.scalar.activation(
+                    out=junk[:],
+                    in_=tv[:, :, e],
+                    func=ACT.Square,
+                    accum_out=nsq[(l, unit)][:, hf, 2 * cb + e : 2 * cb + e + 1],
+                )
+
+        def pw(l, unit):
+            n = 4 if unit == "d" else 8
+            q = nsq[(l, unit)]
+            xx = small.tile([P, n], F32, tag="xx" + unit, name="xx")
+            if unit == "d":
+                nc.gpsimd.tensor_tensor(out=xx[:], in0=q[:, 0, :], in1=q[:, 1, :], op=ALU.add)
+                nc.gpsimd.tensor_scalar_max(out=xx[:], in0=xx[:], scalar1=EPS2)
+            else:
+                nc.gpsimd.tensor_scalar_max(out=xx[:], in0=q[:, 0, :], scalar1=EPS2)
+            r = small.tile([P, n], F32, tag="r" + unit, name="r")
+            nc.gpsimd.tensor_tensor(out=r[:], in0=xx[:], in1=mhalf[:, 0:n], op=ALU.pow)
+            rr[(l, unit)] = r
+
+        def sp(l, unit, hb):
+            r = rr[(l, unit)]
+            rp = pr.tile([P, 512], F32, tag="R", name="rp")
+            for i in range(4):
+                c = 4 * hb + i
+                nc.tensor.transpose(rp[:, i * P : (i + 1) * P], r[:, c : c + 1].to_broadcast([P, P]), ident[:])
+            rbank[(l, unit, hb)] = rp
+
+        def scale_block(eng, dst, w, j0, cb, rsrc):
+            eng.tensor_tensor(
+                out=dst.rearrange("p (e w j) -> p e w j", e=2, w=P, j=4),
+                in0=w[:, j0 : j0 + 4, 256 * cb : 256 * cb + 256].rearrange("p j (w e) -> p e w j", e=2),
+                in1=rsrc.rearrange("p (e w) -> p e w", e=2).unsqueeze(3).to_broadcast([P, 2, P, 4]),
+                op=ALU.mult,
+            )
+
+        def rc(l):
+            t = work.tile([P, 512], F32, tag="rds", name="rds")
+            nc.vector.tensor_copy(out=t[:], in_=rbank[(l, "d", 0)][:])
+            rsb[l] = t
+            gt[(l, "d")] = grp.tile([P, 4 * F], BF16, tag="G", name="dg", align_bytes=64)
+
+        def bd(l, i):
+            c, cb = i // 2, i % 2
+            eng = nc.gpsimd if BD_ENG[i] == "g" else nc.vector
+            scale_block(eng, gt[(l, "d")][:, i * 1024 : (i + 1) * 1024], wt[(l, "d")], 4 * c, cb, rsb[l][:, 256 * cb : 256 * cb + 256])
+
+        def bgu(l, unit, hb):
+            if hb == 0:
+                gt[(l, unit)] = grp.tile([P, 4 * F], BF16, tag="G", name="gg", align_bytes=64)
+            rp = rbank[(l, unit, hb)]
+            for i in range(2):
+                cb = 2 * hb + i
+                scale_block(
+                    nc.vector, gt[(l, unit)][:, cb * 1024 : (cb + 1) * 1024], wt[(l, unit)], 0, cb, rp[:, 256 * i : 256 * i + 256]
+                )
+
+        def cq(l, unit):
+            c = code.tile([P, F], U32, tag="c" + unit, name="cw", align_bytes=64)
+            s = code.tile([P, F], U8, tag="s" + unit, name="cs", align_bytes=64)
+            nc.vector.quantize_mx(out=c[:].bitcast(FP8X4), scales=s[:], in_=gt[(l, unit)][:])
+            cod[(l, unit)] = (c, s)
+
+        def m1(l, c):
+            ups = pm.tile([P, 512], F32, tag="U", name="ups")
+            vps = pm.tile([P, 512], F32, tag="V", name="vps")
+            for dstp, unit in ((vps, "u"), (ups, "g")):
+                cc, ss = cod[(l, unit)]
+                for i in range(4):
+                    t = 4 * c + i
+                    nc.tensor.matmul_mx(
+                        out=dstp[:, i * P : (i + 1) * P],
+                        lhsT=cc[:, t * P : (t + 1) * P].bitcast(FP8X4),
+                        lhsT_scale=ss[:, t * P : (t + 1) * P],
+                        rhs=xc[:, l * B : (l + 1) * B].bitcast(FP8X4),
+                        rhs_scale=xsc[:, l * B : (l + 1) * B],
+                        start=True,
+                        stop=True,
+                    )
+            st[(l, "ups", c)] = ups
+            st[(l, "vps", c)] = vps
+
+        def si(l, c):
+            sil = work.tile([P, 4, B], F32, tag="sil", name="sil")
+            vps = st[(l, "vps", c)]
+            for i in range(4):
+                t = 4 * c + i
+                nc.scalar.activation(out=sil[:, i, :], in_=vps[:, i * P : (i + 1) * P], func=ACT.Silu, scale=sv[:, t : t + 1])
+            st[(l, "sil", c)] = sil
+
+        def stt(l, c):
+            if c == 0:
+                st[(l, "hg")] = work.tile([P, 2 * B * 4], BF16, tag="hg", name="hg", align_bytes=64)
+            hb16 = work.tile([P, 4, B], BF16, tag="hb16", name="hb16")
+            ups = st[(l, "ups", c)]
+            sil = st[(l, "sil", c)]
+            for i in range(4):
+                t = 4 * c + i
+                nc.vector.scalar_tensor_tensor(
+                    out=hb16[:, i, :],
+                    in0=ups[:, i * P : (i + 1) * P],
+                    scalar=su[:, t : t + 1],
+                    in1=sil[:, i, :],
+                    op0=ALU.mult,
+                    op1=ALU.mult,
+                )
+            nc.vector.tensor_copy(
+                out=st[(l, "hg")][:, c * 512 : (c + 1) * 512].rearrange("p (b t) -> p b t", t=4),
+                in_=hb16[:].rearrange("p t b -> p b t"),
+            )
+
+        def ch(l):
+            hc = work.tile([P, 2 * B], U32, tag="hc", name="hc", align_bytes=64)
+            hs = work.tile([P, 2 * B], U8, tag="hs", name="hs", align_bytes=64)
+            nc.vector.quantize_mx(out=hc[:].bitcast(FP8X4), scales=hs[:], in_=st[(l, "hg")][:])
+            st[(l, "hc")] = (hc, hs)
+
+        def m2(l):
+            ops = pm.tile([P, 512], F32, tag="O", name="ops")
+            hc, hs = st[(l, "hc")]
+            dc, ds = cod[(l, "d")]
+            for c in range(2):
+                nc.tensor.matmul_mx(
+                    out=ops[:],
+                    lhsT=hc[:, c * B : (c + 1) * B].bitcast(FP8X4),
+                    lhsT_scale=hs[:, c * B : (c + 1) * B],
+                    rhs=dc[:, c * D : (c + 1) * D].bitcast(FP8X4),
+                    rhs_scale=ds[:, c * D : (c + 1) * D],
+                    start=(c == 0),
+                    stop=(c == 1),
+                )
+            st[(l, "ops")] = ops
+
+        def sq(l):
+            nso = small.tile([P, 1], F32, tag="nso", name="nso")
+            junk = work.tile([P, 512], BF16, tag="junk", name="junk")
+            nc.scalar.activation(out=junk[:], in_=st[(l, "ops")][:], func=ACT.Square, accum_out=nso[:])
+            st[(l, "nso")] = nso
+
+        def po(l):
+            nsx = small.tile([P, 1], F32, tag="nsx", name="nsx")
+            nc.gpsimd.tensor_scalar_max(out=nsx[:], in0=st[(l, "nso")][:], scalar1=EPS2)
+            ro = small.tile([P, 1], F32, tag="ro", name="ro")
+            nc.gpsimd.tensor_tensor(out=ro[:], in0=nsx[:], in1=mhalf[:, 0:1], op=ALU.pow)
+            st[(l, "ro")] = ro
+
+        def cp(l):
+            ob = work.tile([P, D], F32, tag="ob", name="ob")
+            nc.scalar.activation(
+                out=ob[:].rearrange("p (cb w e) -> p cb w e", cb=2, w=P, e=2),
+                in_=st[(l, "ops")][:].rearrange("p (cb e w) -> p cb w e", cb=2, e=2, w=P),
+                func=ACT.Copy,
+                scale=st[(l, "ro")][:],
+            )
+            nc.sync.dma_start(out=out[:, l, :], in_=ob[:])
+
+        for unit in ("d", "g", "u"):
+            load(0, unit)
+        load_x()
+        for it in range(L + 2):
+            a, b, m = it, it - 1, it - 2
+            ha, hb_, hm = a < L, 0 <= b < L, 0 <= m < L
+
+            def A(k):
+                if ha:
+                    a_item(a, k)
+
+            if a + 1 < L:
+                for unit in ("d", "g", "u"):
+                    load(a + 1, unit)
+            if hm:
+                m1(m, 0)
+            if hb_:
+                rc(b)
+                bd(b, 0)
+            A(0)
+            A(1)
+            if hb_:
+                bgu(b, "g", 0)
+            if hm:
+                si(m, 0)
+            A(2)
+            if hb_:
+                sp(b, "g", 1)
+                bd(b, 1)
+            if hm:
+                stt(m, 0)
+            A(3)
+            if ha:
+                pw(a, "d")
+            if hb_:
+                bgu(b, "g", 1)
+            A(4)
+            A(5)
+            if hm:
+                m1(m, 1)
+            if hb_:
+                sp(b, "u", 0)
+            if hm:
+                si(m, 1)
+            if hb_:
+                bd(b, 2)
+                bgu(b, "u", 0)
+            A(6)
+            if hb_:
+                cq(b, "g")
+            A(7)
+            if hb_:
+                bd(b, 3)
+            if ha:
+                pw(a, "g")
+            if hm:
+                stt(m, 1)
+                ch(m)
+            if hb_:
+                sp(b, "u", 1)
+            A(8)
+            if hb_:
+                bgu(b, "u", 1)
+            A(9)
+            A(10)
+            if hm:
+                m2(m)
+                sq(m)
+                po(m)
+            if hb_:
+                cq(b, "u")
+            if ha:
+                sp(a, "d", 0)
+            A(11)
+            if ha:
+                pw(a, "u")
+            if hm:
+                cp(m)
+            if hb_:
+                cq(b, "d")
+            if ha:
+                sp(a, "g", 0)
+            if it == 0:
+                prep_x()

@@ -17,7 +17,7 @@ B, L, D, F = 128, 8, 512, 1024
 FLOPS = 2 * B * L * (D * F * 2 + F * D)
 EPS2 = 1e-24
 MANUAL = True
-BD_ENG = ['g','g','g','g']
+BD_ENG = ['v','v','v','v']
 
 
 def tile_npertokenswishglu_kernel(tc, x, W_gate, W_up, W_down, s_u, s_v, out):

@@ -17,7 +17,7 @@ B, L, D, F = 128, 8, 512, 1024
 FLOPS = 2 * B * L * (D * F * 2 + F * D)
 EPS2 = 1e-24
 MANUAL = True
-BD_ENG = ['v','v','v','v']
+BD_ENG = ['v','v','g','g']
 
 
 def tile_npertokenswishglu_kernel(tc, x, W_gate, W_up, W_down, s_u, s_v, out):
@@ -39,7 +39,9 @@ def tile_npertokenswishglu_kernel(tc, x, W_gate, W_up, W_down, s_u, s_v, out):
         make_identity(nc, ident[:])
         mhalf = const.tile([P, 8], F32)
         nc.vector.memset(mhalf[:], -0.5)
-        gz = const.tile([P, P], F32)
+        identb = const.tile([P, P], BF16)
+        make_identity(nc, identb[:])
+        gz = const.tile([P, P], BF16)
         nc.vector.memset(gz[:], 0.0)
         xs = const.tile([P, L, D], BF16)
         xg = const.tile([P, L * B * 4], BF16, align_bytes=64)
@@ -61,8 +63,8 @@ def tile_npertokenswishglu_kernel(tc, x, W_gate, W_up, W_down, s_u, s_v, out):
             if unit == "d":
                 t = wpool.tile([P, 8, D], BF16, tag="W", name="wd")
                 nc.sync.dma_start(
-                    out=t[:].rearrange("p (g e) n -> p g (e n)", g=4),
-                    in_=W_down[l].rearrange("(g p e) n -> p g (e n)", g=4, p=P, e=2),
+                    out=t[:],
+                    in_=W_down[l].rearrange("(g p) n -> p g n", g=8, p=P),
                 )
             else:
                 W = W_gate if unit == "g" else W_up
@@ -75,8 +77,8 @@ def tile_npertokenswishglu_kernel(tc, x, W_gate, W_up, W_down, s_u, s_v, out):
 
         def load_x():
             nc.sync.dma_start(out=xs[:], in_=x)
-            nc.sync.dma_start(out=gz[0:4, :], in_=s_u.bitcast(F32).rearrange("o (c w) -> (o c) w", c=4))
-            nc.sync.dma_start(out=gz[4:8, :], in_=s_v.bitcast(F32).rearrange("o (c w) -> (o c) w", c=4))
+            nc.sync.dma_start(out=gz[0:8, :], in_=s_u.rearrange("o (t p) -> (o t) p", t=8))
+            nc.sync.dma_start(out=gz[8:16, :], in_=s_v.rearrange("o (t p) -> (o t) p", t=8))
 
         def prep_x():
             xw = xs[:].bitcast(F32)
@@ -94,10 +96,10 @@ def tile_npertokenswishglu_kernel(tc, x, W_gate, W_up, W_down, s_u, s_v, out):
                     out=xgw[:, 2 * lp : 2 * lp + 2, :, :],
                     in_=xt[:].rearrange("p (i u b) -> p i b u", i=2, u=2, b=B),
                 )
-            gp = pt.tile([P, 512], F32, tag="T", name="gp")
-            nc.tensor.transpose(gp[:, 0:P], gz[:], ident[:])
-            nc.scalar.activation(out=su[:], in_=gp[:, 0:4].bitcast(BF16), func=ACT.Abs)
-            nc.scalar.activation(out=sv[:], in_=gp[:, 4:8].bitcast(BF16), func=ACT.Abs, scale=math.sqrt(D))
+            gp = pt.tile([P, 1024], BF16, tag="T", name="gp")
+            nc.tensor.transpose(gp[:, 0:P], gz[:], identb[:])
+            nc.scalar.activation(out=su[:], in_=gp[:, 0:8], func=ACT.Abs)
+            nc.scalar.activation(out=sv[:], in_=gp[:, 8:16], func=ACT.Abs, scale=math.sqrt(D))
             nc.vector.quantize_mx(out=xc[:].bitcast(FP8X4), scales=xsc[:], in_=xg[:])
 
         def a_item(l, k):
@@ -147,22 +149,23 @@ def tile_npertokenswishglu_kernel(tc, x, W_gate, W_up, W_down, s_u, s_v, out):
 
         def scale_block(eng, dst, w, j0, cb, rsrc):
             eng.tensor_tensor(
-                out=dst.rearrange("p (e w j) -> p e w j", e=2, w=P, j=4),
-                in0=w[:, j0 : j0 + 4, 256 * cb : 256 * cb + 256].rearrange("p j (w e) -> p e w j", e=2),
-                in1=rsrc.rearrange("p (e w) -> p e w", e=2).unsqueeze(3).to_broadcast([P, 2, P, 4]),
+                out=dst.rearrange("p (w e j) -> p w j e", w=P, e=2, j=4),
+                in0=w[:, j0 : j0 + 4, 256 * cb : 256 * cb + 256].rearrange("p j (w e) -> p w j e", e=2),
+                in1=rsrc.rearrange("p (e w) -> p w e", e=2).unsqueeze(2).to_broadcast([P, P, 4, 2]),
                 op=ALU.mult,
             )
 
         def rc(l):
             t = work.tile([P, 512], F32, tag="rds", name="rds")
-            nc.vector.tensor_copy(out=t[:], in_=rbank[(l, "d", 0)][:])
+            nc.scalar.copy(out=t[:], in_=rbank[(l, "d", 0)][:])
             rsb[l] = t
             gt[(l, "d")] = grp.tile([P, 4 * F], BF16, tag="G", name="dg", align_bytes=64)
 
         def bd(l, i):
             c, cb = i // 2, i % 2
             eng = nc.gpsimd if BD_ENG[i] == "g" else nc.vector
-            scale_block(eng, gt[(l, "d")][:, i * 1024 : (i + 1) * 1024], wt[(l, "d")], 4 * c, cb, rsb[l][:, 256 * cb : 256 * cb + 256])
+            rsrc = rsb[l] if BD_ENG[i] == "g" else rbank[(l, "d", 0)]
+            scale_block(eng, gt[(l, "d")][:, i * 1024 : (i + 1) * 1024], wt[(l, "d")], 4 * c, cb, rsrc[:, 256 * cb : 256 * cb + 256])
 
         def bgu(l, unit, hb):
             if hb == 0:
@@ -266,8 +269,8 @@ def tile_npertokenswishglu_kernel(tc, x, W_gate, W_up, W_down, s_u, s_v, out):
         def cp(l):
             ob = work.tile([P, D], F32, tag="ob", name="ob")
             nc.scalar.activation(
-                out=ob[:].rearrange("p (cb w e) -> p cb w e", cb=2, w=P, e=2),
-                in_=st[(l, "ops")][:].rearrange("p (cb e w) -> p cb w e", cb=2, e=2, w=P),
+                out=ob[:],
+                in_=st[(l, "ops")][:],
                 func=ACT.Copy,
                 scale=st[(l, "ro")][:],
             )
@@ -292,6 +295,8 @@ def tile_npertokenswishglu_kernel(tc, x, W_gate, W_up, W_down, s_u, s_v, out):
             if hb_:
                 rc(b)
                 bd(b, 0)
+                bd(b, 1)
+                bd(b, 2)
             A(0)
             A(1)
             if hb_:
@@ -299,12 +304,11 @@ def tile_npertokenswishglu_kernel(tc, x, W_gate, W_up, W_down, s_u, s_v, out):
             if hm:
                 si(m, 0)
             A(2)
-            if hb_:
-                sp(b, "g", 1)
-                bd(b, 1)
             if hm:
                 stt(m, 0)
             A(3)
+            if hb_:
+                sp(b, "g", 1)
             if ha:
                 pw(a, "d")
             if hb_:
@@ -318,14 +322,12 @@ def tile_npertokenswishglu_kernel(tc, x, W_gate, W_up, W_down, s_u, s_v, out):
             if hm:
                 si(m, 1)
             if hb_:
-                bd(b, 2)
+                bd(b, 3)
                 bgu(b, "u", 0)
             A(6)
             if hb_:
                 cq(b, "g")
             A(7)
-            if hb_:
-                bd(b, 3)
             if ha:
                 pw(a, "g")
             if hm:

@@ -16,8 +16,6 @@ P = 128
 B, L, D, F = 128, 8, 512, 1024
 FLOPS = 2 * B * L * (D * F * 2 + F * D)
 EPS2 = 1e-24
-MANUAL = True
-BD_ENG = ['v','v','g','g']
 
 
 def tile_npertokenswishglu_kernel(tc, x, W_gate, W_up, W_down, s_u, s_v, out):
@@ -32,15 +30,14 @@ def tile_npertokenswishglu_kernel(tc, x, W_gate, W_up, W_down, s_u, s_v, out):
         pt = ctx.enter_context(tc.psum_pool(name="pt", bufs=3))
         pr = ctx.enter_context(tc.psum_pool(name="pr", bufs=2))
         pm = ctx.enter_context(tc.psum_pool(name="pm", bufs=1))
-        if MANUAL:
-            ctx.enter_context(tc.manual_schedule())
+        ctx.enter_context(tc.manual_schedule())
 
         ident = const.tile([P, P], F32)
         make_identity(nc, ident[:])
-        mhalf = const.tile([P, 8], F32)
-        nc.vector.memset(mhalf[:], -0.5)
         identb = const.tile([P, P], BF16)
         make_identity(nc, identb[:])
+        mhalf = const.tile([P, 8], F32)
+        nc.vector.memset(mhalf[:], -0.5)
         gz = const.tile([P, P], BF16)
         nc.vector.memset(gz[:], 0.0)
         xs = const.tile([P, L, D], BF16)
@@ -62,10 +59,7 @@ def tile_npertokenswishglu_kernel(tc, x, W_gate, W_up, W_down, s_u, s_v, out):
         def load(l, unit):
             if unit == "d":
                 t = wpool.tile([P, 8, D], BF16, tag="W", name="wd")
-                nc.sync.dma_start(
-                    out=t[:],
-                    in_=W_down[l].rearrange("(g p) n -> p g n", g=8, p=P),
-                )
+                nc.sync.dma_start(out=t[:], in_=W_down[l].rearrange("(g p) n -> p g n", g=8, p=P))
             else:
                 W = W_gate if unit == "g" else W_up
                 t = wpool.tile([P, 4, F], BF16, tag="W", name="wg")
@@ -84,7 +78,7 @@ def tile_npertokenswishglu_kernel(tc, x, W_gate, W_up, W_down, s_u, s_v, out):
             xw = xs[:].bitcast(F32)
             xgw = xg[:].bitcast(F32).rearrange("p (l b u) -> p l b u", l=L, b=B, u=2)
             for lp in range(L // 2):
-                xt = pt.tile([P, 512], F32, tag="T", name="xt")
+                xt = pm.tile([P, 512], F32, tag="UV"[lp % 2], name="xt")
                 for i in range(2):
                     for u in range(2):
                         nc.tensor.transpose(
@@ -96,7 +90,7 @@ def tile_npertokenswishglu_kernel(tc, x, W_gate, W_up, W_down, s_u, s_v, out):
                     out=xgw[:, 2 * lp : 2 * lp + 2, :, :],
                     in_=xt[:].rearrange("p (i u b) -> p i b u", i=2, u=2, b=B),
                 )
-            gp = pt.tile([P, 1024], BF16, tag="T", name="gp")
+            gp = pm.tile([P, 1024], BF16, tag="O", name="gp")
             nc.tensor.transpose(gp[:, 0:P], gz[:], identb[:])
             nc.scalar.activation(out=su[:], in_=gp[:, 0:8], func=ACT.Abs)
             nc.scalar.activation(out=sv[:], in_=gp[:, 8:16], func=ACT.Abs, scale=math.sqrt(D))
@@ -142,16 +136,18 @@ def tile_npertokenswishglu_kernel(tc, x, W_gate, W_up, W_down, s_u, s_v, out):
         def sp(l, unit, hb):
             r = rr[(l, unit)]
             rp = pr.tile([P, 512], F32, tag="R", name="rp")
-            for i in range(4):
-                c = 4 * hb + i
-                nc.tensor.transpose(rp[:, i * P : (i + 1) * P], r[:, c : c + 1].to_broadcast([P, P]), ident[:])
+            for e in range(2):
+                for i in range(2):
+                    c = 2 * (2 * hb + i) + e
+                    o = (2 * e + i) * P
+                    nc.tensor.transpose(rp[:, o : o + P], r[:, c : c + 1].to_broadcast([P, P]), ident[:])
             rbank[(l, unit, hb)] = rp
 
-        def scale_block(eng, dst, w, j0, cb, rsrc):
+        def scale(eng, dst, w, j0, n0, rsrc, q0, nq):
             eng.tensor_tensor(
-                out=dst.rearrange("p (w e j) -> p w j e", w=P, e=2, j=4),
-                in0=w[:, j0 : j0 + 4, 256 * cb : 256 * cb + 256].rearrange("p j (w e) -> p w j e", e=2),
-                in1=rsrc.rearrange("p (e w) -> p w e", e=2).unsqueeze(2).to_broadcast([P, P, 4, 2]),
+                out=dst.rearrange("p (q e j) -> p q j e", q=nq, e=2, j=4),
+                in0=w[:, j0 : j0 + 4, n0 : n0 + 2 * nq].rearrange("p j (q e) -> p q j e", e=2),
+                in1=rsrc.rearrange("p (e q) -> p q e", e=2)[:, q0 : q0 + nq, :].unsqueeze(2).to_broadcast([P, nq, 4, 2]),
                 op=ALU.mult,
             )
 
@@ -159,23 +155,23 @@ def tile_npertokenswishglu_kernel(tc, x, W_gate, W_up, W_down, s_u, s_v, out):
             t = work.tile([P, 512], F32, tag="rds", name="rds")
             nc.scalar.copy(out=t[:], in_=rbank[(l, "d", 0)][:])
             rsb[l] = t
+
+        def bd_alloc(l):
             gt[(l, "d")] = grp.tile([P, 4 * F], BF16, tag="G", name="dg", align_bytes=64)
 
-        def bd(l, i):
-            c, cb = i // 2, i % 2
-            eng = nc.gpsimd if BD_ENG[i] == "g" else nc.vector
-            rsrc = rsb[l] if BD_ENG[i] == "g" else rbank[(l, "d", 0)]
-            scale_block(eng, gt[(l, "d")][:, i * 1024 : (i + 1) * 1024], wt[(l, "d")], 4 * c, cb, rsrc[:, 256 * cb : 256 * cb + 256])
+        def bd_v(l, c):
+            scale(nc.vector, gt[(l, "d")][:, c * 2048 : (c + 1) * 2048], wt[(l, "d")], 4 * c, 0, rbank[(l, "d", 0)][:], 0, 256)
+
+        def bd_g(l, c, i):
+            o = c * 2048 + i * 1024
+            scale(nc.gpsimd, gt[(l, "d")][:, o : o + 1024], wt[(l, "d")], 4 * c, 256 * i, rsb[l][:], 128 * i, 128)
 
         def bgu(l, unit, hb):
             if hb == 0:
                 gt[(l, unit)] = grp.tile([P, 4 * F], BF16, tag="G", name="gg", align_bytes=64)
-            rp = rbank[(l, unit, hb)]
-            for i in range(2):
-                cb = 2 * hb + i
-                scale_block(
-                    nc.vector, gt[(l, unit)][:, cb * 1024 : (cb + 1) * 1024], wt[(l, unit)], 0, cb, rp[:, 256 * i : 256 * i + 256]
-                )
+            scale(
+                nc.vector, gt[(l, unit)][:, hb * 2048 : (hb + 1) * 2048], wt[(l, unit)], 0, 512 * hb, rbank[(l, unit, hb)][:], 0, 256
+            )
 
         def cq(l, unit):
             c = code.tile([P, F], U32, tag="c" + unit, name="cw", align_bytes=64)
@@ -211,8 +207,6 @@ def tile_npertokenswishglu_kernel(tc, x, W_gate, W_up, W_down, s_u, s_v, out):
             st[(l, "sil", c)] = sil
 
         def stt(l, c):
-            if c == 0:
-                st[(l, "hg")] = work.tile([P, 2 * B * 4], BF16, tag="hg", name="hg", align_bytes=64)
             hb16 = work.tile([P, 4, B], BF16, tag="hb16", name="hb16")
             ups = st[(l, "ups", c)]
             sil = st[(l, "sil", c)]
@@ -226,9 +220,18 @@ def tile_npertokenswishglu_kernel(tc, x, W_gate, W_up, W_down, s_u, s_v, out):
                     op0=ALU.mult,
                     op1=ALU.mult,
                 )
-            nc.vector.tensor_copy(
+            st[(l, "hb16", c)] = hb16
+
+        def rg(l, c):
+            if c == 0:
+                st[(l, "hg")] = work.tile([P, 2 * B * 4], BF16, tag="hg", name="hg", align_bytes=64)
+            nc.gpsimd.tensor_scalar(
                 out=st[(l, "hg")][:, c * 512 : (c + 1) * 512].rearrange("p (b t) -> p b t", t=4),
-                in_=hb16[:].rearrange("p t b -> p b t"),
+                in0=st[(l, "hb16", c)][:].rearrange("p t b -> p b t"),
+                scalar1=1.0,
+                scalar2=0.0,
+                op0=ALU.mult,
+                op1=ALU.add,
             )
 
         def ch(l):
@@ -268,20 +271,18 @@ def tile_npertokenswishglu_kernel(tc, x, W_gate, W_up, W_down, s_u, s_v, out):
 
         def cp(l):
             ob = work.tile([P, D], F32, tag="ob", name="ob")
-            nc.scalar.activation(
-                out=ob[:],
-                in_=st[(l, "ops")][:],
-                func=ACT.Copy,
-                scale=st[(l, "ro")][:],
-            )
+            nc.scalar.activation(out=ob[:], in_=st[(l, "ops")][:], func=ACT.Copy, scale=st[(l, "ro")][:])
             nc.sync.dma_start(out=out[:, l, :], in_=ob[:])
 
-        for unit in ("d", "g", "u"):
-            load(0, unit)
+        load(0, "d")
         load_x()
-        for it in range(L + 2):
+        load(0, "g")
+        load(0, "u")
+        for it in range(L + 3):
             a, b, m = it, it - 1, it - 2
             ha, hb_, hm = a < L, 0 <= b < L, 0 <= m < L
+            first = it == 0
+            lastb = b == L - 1
 
             def A(k):
                 if ha:
@@ -292,20 +293,31 @@ def tile_npertokenswishglu_kernel(tc, x, W_gate, W_up, W_down, s_u, s_v, out):
                     load(a + 1, unit)
             if hm:
                 m1(m, 0)
-            if hb_:
+            if hb_ and b > 0:
                 rc(b)
-                bd(b, 0)
-                bd(b, 1)
-                bd(b, 2)
+            if hb_:
+                bd_alloc(b)
+                if lastb:
+                    bd_g(b, 0, 0)
+                    bd_g(b, 0, 1)
+                else:
+                    bd_v(b, 0)
+                bd_g(b, 1, 0)
+                bd_g(b, 1, 1)
             A(0)
+            if 0 <= m - 1 < L:
+                cp(m - 1)
             A(1)
             if hb_:
                 bgu(b, "g", 0)
             if hm:
                 si(m, 0)
             A(2)
+            if first:
+                prep_x()
             if hm:
                 stt(m, 0)
+                rg(m, 0)
             A(3)
             if hb_:
                 sp(b, "g", 1)
@@ -315,6 +327,11 @@ def tile_npertokenswishglu_kernel(tc, x, W_gate, W_up, W_down, s_u, s_v, out):
                 bgu(b, "g", 1)
             A(4)
             A(5)
+            if first:
+                sp(a, "d", 0)
+            A(6)
+            if first:
+                rc(a)
             if hm:
                 m1(m, 1)
             if hb_:
@@ -322,40 +339,37 @@ def tile_npertokenswishglu_kernel(tc, x, W_gate, W_up, W_down, s_u, s_v, out):
             if hm:
                 si(m, 1)
             if hb_:
-                bd(b, 3)
                 bgu(b, "u", 0)
-            A(6)
-            if hb_:
                 cq(b, "g")
             A(7)
             if ha:
                 pw(a, "g")
             if hm:
                 stt(m, 1)
-                ch(m)
+                rg(m, 1)
             if hb_:
                 sp(b, "u", 1)
             A(8)
             if hb_:
                 bgu(b, "u", 1)
             A(9)
+            if first:
+                sp(a, "g", 0)
             A(10)
+            if hm:
+                ch(m)
+            if hb_:
+                cq(b, "u")
+            if ha and not first:
+                sp(a, "d", 0)
+            A(11)
             if hm:
                 m2(m)
                 sq(m)
                 po(m)
-            if hb_:
-                cq(b, "u")
-            if ha:
-                sp(a, "d", 0)
-            A(11)
             if ha:
                 pw(a, "u")
-            if hm:
-                cp(m)
             if hb_:
                 cq(b, "d")
-            if ha:
+            if ha and not first:
                 sp(a, "g", 0)
-            if it == 0:
-                prep_x()

@@ -48,6 +48,7 @@ def tile_npertokenswishglu_kernel(tc, x, W_gate, W_up, W_down, s_u, s_v, out):
         sv = const.tile([P, 8], F32)
 
         wt = {}
+        tbank = {}
         nsq = {}
         rr = {}
         rbank = {}
@@ -96,21 +97,27 @@ def tile_npertokenswishglu_kernel(tc, x, W_gate, W_up, W_down, s_u, s_v, out):
             nc.scalar.activation(out=sv[:], in_=gp[:, 8:16], func=ACT.Abs, scale=math.sqrt(D))
             nc.vector.quantize_mx(out=xc[:].bitcast(FP8X4), scales=xsc[:], in_=xg[:])
 
-        def a_item(l, k):
+        def which(k):
             if k < 4:
-                unit, cb, hf = "d", k // 2, k % 2
-            elif k < 8:
-                unit, cb, hf = "g", k - 4, 0
-            else:
-                unit, cb, hf = "u", k - 8, 0
-            if k % 4 == 0:
-                shape = [P, 2, 4] if unit == "d" else [P, 1, 8]
-                nsq[(l, unit)] = small.tile(shape, F32, tag="nsq" + unit, name="nsq")
+                return "d", k // 2, k % 2
+            if k < 8:
+                return "g", k - 4, 0
+            return "u", k - 8, 0
+
+        def a_t(l, k):
+            unit, cb, hf = which(k)
             ww = wt[(l, unit)][:].bitcast(F32)
             tp = pt.tile([P, 512], F32, tag="T", name="tp")
             for j in range(4):
                 nc.tensor.transpose(tp[:, j * P : (j + 1) * P], ww[:, 4 * hf + j, cb * P : (cb + 1) * P], ident[:])
-            tv = tp[:].bitcast(BF16).rearrange("p (k e) -> p k e", e=2)
+            tbank[(l, k)] = tp
+
+        def a_s(l, k):
+            unit, cb, hf = which(k)
+            if k % 4 == 0:
+                shape = [P, 2, 4] if unit == "d" else [P, 1, 8]
+                nsq[(l, unit)] = small.tile(shape, F32, tag="nsq" + unit, name="nsq")
+            tv = tbank[(l, k)][:].bitcast(BF16).rearrange("p (k e) -> p k e", e=2)
             for e in range(2):
                 junk = work.tile([P, 512], BF16, tag="junk", name="junk")
                 nc.scalar.activation(
@@ -159,8 +166,8 @@ def tile_npertokenswishglu_kernel(tc, x, W_gate, W_up, W_down, s_u, s_v, out):
         def bd_alloc(l):
             gt[(l, "d")] = grp.tile([P, 4 * F], BF16, tag="G", name="dg", align_bytes=64)
 
-        def bd_v(l, c):
-            scale(nc.vector, gt[(l, "d")][:, c * 2048 : (c + 1) * 2048], wt[(l, "d")], 4 * c, 0, rbank[(l, "d", 0)][:], 0, 256)
+        def bd_v(l):
+            scale(nc.vector, gt[(l, "d")][:, 0:1024], wt[(l, "d")], 0, 0, rbank[(l, "d", 0)][:], 0, 128)
 
         def bd_g(l, c, i):
             o = c * 2048 + i * 1024
@@ -274,102 +281,90 @@ def tile_npertokenswishglu_kernel(tc, x, W_gate, W_up, W_down, s_u, s_v, out):
             nc.scalar.activation(out=ob[:], in_=st[(l, "ops")][:], func=ACT.Copy, scale=st[(l, "ro")][:])
             nc.sync.dma_start(out=out[:, l, :], in_=ob[:])
 
-        load(0, "d")
-        load_x()
-        load(0, "g")
-        load(0, "u")
-        for it in range(L + 3):
-            a, b, m = it, it - 1, it - 2
-            ha, hb_, hm = a < L, 0 <= b < L, 0 <= m < L
-            first = it == 0
-            lastb = b == L - 1
+        def on(l):
+            return 0 <= l < L
 
-            def A(k):
-                if ha:
-                    a_item(a, k)
-
-            if a + 1 < L:
+        for it in range(-1, L + 3):
+            a, p, q, r = it, it - 1, it - 2, it - 3
+            if on(a + 1):
                 for unit in ("d", "g", "u"):
                     load(a + 1, unit)
-            if hm:
-                m1(m, 0)
-            if hb_ and b > 0:
-                rc(b)
-            if hb_:
-                bd_alloc(b)
-                if lastb:
-                    bd_g(b, 0, 0)
-                    bd_g(b, 0, 1)
+                if a + 1 == 0:
+                    load_x()
+            for k in range(12):
+                if k == 0 and on(p):
+                    rc(p)
+                if on(a):
+                    a_s(a, k)
+                nl, nk = (a, k + 2) if k + 2 < 12 else (a + 1, k - 10)
+                if on(nl):
+                    a_t(nl, nk)
+                if k == 0:
+                    if on(p):
+                        bd_alloc(p)
+                        bd_v(p)
+                        bd_g(p, 0, 1)
+                    if on(q):
+                        m1(q, 0)
+                elif k == 1:
+                    if on(p):
+                        bgu(p, "g", 0)
+                        sp(p, "g", 1)
+                        bd_g(p, 1, 0)
+                elif k == 2:
+                    if on(q):
+                        si(q, 0)
+                elif k == 3:
+                    if on(p):
+                        bgu(p, "g", 1)
+                        sp(p, "u", 0)
+                        bd_g(p, 1, 1)
+                elif k == 4:
+                    if on(q):
+                        stt(q, 0)
+                        rg(q, 0)
+                    if on(r):
+                        m2(r)
+                elif k == 5:
+                    if on(p):
+                        bgu(p, "u", 0)
+                    if on(q):
+                        m1(q, 1)
+                    if on(r):
+                        sq(r)
+                elif k == 6:
+                    if on(p):
+                        sp(p, "u", 1)
+                    if on(a):
+                        pw(a, "d")
+                    if on(r):
+                        po(r)
+                elif k == 7:
+                    if on(q):
+                        si(q, 1)
+                elif k == 8:
+                    if on(q):
+                        stt(q, 1)
+                        rg(q, 1)
+                    if on(p):
+                        bgu(p, "u", 1)
+                    if on(r):
+                        cp(r)
+                elif k == 9:
+                    if on(a):
+                        sp(a, "d", 0)
+                        pw(a, "g")
+                elif k == 10:
+                    if on(p):
+                        cq(p, "g")
+                        cq(p, "u")
                 else:
-                    bd_v(b, 0)
-                bd_g(b, 1, 0)
-                bd_g(b, 1, 1)
-            A(0)
-            if 0 <= m - 1 < L:
-                cp(m - 1)
-            A(1)
-            if hb_:
-                bgu(b, "g", 0)
-            if hm:
-                si(m, 0)
-            A(2)
-            if first:
-                prep_x()
-            if hm:
-                stt(m, 0)
-                rg(m, 0)
-            A(3)
-            if hb_:
-                sp(b, "g", 1)
-            if ha:
-                pw(a, "d")
-            if hb_:
-                bgu(b, "g", 1)
-            A(4)
-            A(5)
-            if first:
-                sp(a, "d", 0)
-            A(6)
-            if first:
-                rc(a)
-            if hm:
-                m1(m, 1)
-            if hb_:
-                sp(b, "u", 0)
-            if hm:
-                si(m, 1)
-            if hb_:
-                bgu(b, "u", 0)
-                cq(b, "g")
-            A(7)
-            if ha:
-                pw(a, "g")
-            if hm:
-                stt(m, 1)
-                rg(m, 1)
-            if hb_:
-                sp(b, "u", 1)
-            A(8)
-            if hb_:
-                bgu(b, "u", 1)
-            A(9)
-            if first:
-                sp(a, "g", 0)
-            A(10)
-            if hm:
-                ch(m)
-            if hb_:
-                cq(b, "u")
-            if ha and not first:
-                sp(a, "d", 0)
-            A(11)
-            if hm:
-                m2(m)
-                sq(m)
-                po(m)
-            if ha:
-                pw(a, "u")
-            if hb_:
-                cq(b, "d")
-            if ha and not first:
-                sp(a, "g", 0)
+                    if on(p):
+                        cq(p, "d")
+                    if on(q):
+                        ch(q)
+                    if on(a):
+                        sp(a, "g", 0)
+                        pw(a, "u")
+                    if a == 0:
+                        prep_x()

@@ -16,6 +16,8 @@ P = 128
 B, L, D, F = 128, 8, 512, 1024
 FLOPS = 2 * B * L * (D * F * 2 + F * D)
 EPS2 = 1e-24
+MANUAL = True
+BD_ENG = ['v','v','g','g']
 
 
 def tile_npertokenswishglu_kernel(tc, x, W_gate, W_up, W_down, s_u, s_v, out):
@@ -30,14 +32,15 @@ def tile_npertokenswishglu_kernel(tc, x, W_gate, W_up, W_down, s_u, s_v, out):
         pt = ctx.enter_context(tc.psum_pool(name="pt", bufs=3))
         pr = ctx.enter_context(tc.psum_pool(name="pr", bufs=2))
         pm = ctx.enter_context(tc.psum_pool(name="pm", bufs=1))
-        ctx.enter_context(tc.manual_schedule())
+        if MANUAL:
+            ctx.enter_context(tc.manual_schedule())
 
         ident = const.tile([P, P], F32)
         make_identity(nc, ident[:])
-        identb = const.tile([P, P], BF16)
-        make_identity(nc, identb[:])
         mhalf = const.tile([P, 8], F32)
         nc.vector.memset(mhalf[:], -0.5)
+        identb = const.tile([P, P], BF16)
+        make_identity(nc, identb[:])
         gz = const.tile([P, P], BF16)
         nc.vector.memset(gz[:], 0.0)
         xs = const.tile([P, L, D], BF16)
@@ -48,7 +51,6 @@ def tile_npertokenswishglu_kernel(tc, x, W_gate, W_up, W_down, s_u, s_v, out):
         sv = const.tile([P, 8], F32)
 
         wt = {}
-        tbank = {}
         nsq = {}
         rr = {}
         rbank = {}
@@ -60,7 +62,10 @@ def tile_npertokenswishglu_kernel(tc, x, W_gate, W_up, W_down, s_u, s_v, out):
         def load(l, unit):
             if unit == "d":
                 t = wpool.tile([P, 8, D], BF16, tag="W", name="wd")
-                nc.sync.dma_start(out=t[:], in_=W_down[l].rearrange("(g p) n -> p g n", g=8, p=P))
+                nc.sync.dma_start(
+                    out=t[:],
+                    in_=W_down[l].rearrange("(g p) n -> p g n", g=8, p=P),
+                )
             else:
                 W = W_gate if unit == "g" else W_up
                 t = wpool.tile([P, 4, F], BF16, tag="W", name="wg")
@@ -79,7 +84,7 @@ def tile_npertokenswishglu_kernel(tc, x, W_gate, W_up, W_down, s_u, s_v, out):
             xw = xs[:].bitcast(F32)
             xgw = xg[:].bitcast(F32).rearrange("p (l b u) -> p l b u", l=L, b=B, u=2)
             for lp in range(L // 2):
-                xt = pm.tile([P, 512], F32, tag="UV"[lp % 2], name="xt")
+                xt = pt.tile([P, 512], F32, tag="T", name="xt")
                 for i in range(2):
                     for u in range(2):
                         nc.tensor.transpose(
@@ -91,33 +96,27 @@ def tile_npertokenswishglu_kernel(tc, x, W_gate, W_up, W_down, s_u, s_v, out):
                     out=xgw[:, 2 * lp : 2 * lp + 2, :, :],
                     in_=xt[:].rearrange("p (i u b) -> p i b u", i=2, u=2, b=B),
                 )
-            gp = pm.tile([P, 1024], BF16, tag="O", name="gp")
+            gp = pt.tile([P, 1024], BF16, tag="T", name="gp")
             nc.tensor.transpose(gp[:, 0:P], gz[:], identb[:])
             nc.scalar.activation(out=su[:], in_=gp[:, 0:8], func=ACT.Abs)
             nc.scalar.activation(out=sv[:], in_=gp[:, 8:16], func=ACT.Abs, scale=math.sqrt(D))
             nc.vector.quantize_mx(out=xc[:].bitcast(FP8X4), scales=xsc[:], in_=xg[:])
 
-        def which(k):
+        def a_item(l, k):
             if k < 4:
-                return "d", k // 2, k % 2
-            if k < 8:
-                return "g", k - 4, 0
-            return "u", k - 8, 0
-
-        def a_t(l, k):
-            unit, cb, hf = which(k)
+                unit, cb, hf = "d", k // 2, k % 2
+            elif k < 8:
+                unit, cb, hf = "g", k - 4, 0
+            else:
+                unit, cb, hf = "u", k - 8, 0
+            if k % 4 == 0:
+                shape = [P, 2, 4] if unit == "d" else [P, 1, 8]
+                nsq[(l, unit)] = small.tile(shape, F32, tag="nsq" + unit, name="nsq")
             ww = wt[(l, unit)][:].bitcast(F32)
             tp = pt.tile([P, 512], F32, tag="T", name="tp")
             for j in range(4):
                 nc.tensor.transpose(tp[:, j * P : (j + 1) * P], ww[:, 4 * hf + j, cb * P : (cb + 1) * P], ident[:])
-            tbank[(l, k)] = tp
-
-        def a_s(l, k):
-            unit, cb, hf = which(k)
-            if k % 4 == 0:
-                shape = [P, 2, 4] if unit == "d" else [P, 1, 8]
-                nsq[(l, unit)] = small.tile(shape, F32, tag="nsq" + unit, name="nsq")
-            tv = tbank[(l, k)][:].bitcast(BF16).rearrange("p (k e) -> p k e", e=2)
+            tv = tp[:].bitcast(BF16).rearrange("p (k e) -> p k e", e=2)
             for e in range(2):
                 junk = work.tile([P, 512], BF16, tag="junk", name="junk")
                 nc.scalar.activation(
@@ -143,18 +142,25 @@ def tile_npertokenswishglu_kernel(tc, x, W_gate, W_up, W_down, s_u, s_v, out):
         def sp(l, unit, hb):
             r = rr[(l, unit)]
             rp = pr.tile([P, 512], F32, tag="R", name="rp")
-            for e in range(2):
-                for i in range(2):
-                    c = 2 * (2 * hb + i) + e
-                    o = (2 * e + i) * P
-                    nc.tensor.transpose(rp[:, o : o + P], r[:, c : c + 1].to_broadcast([P, P]), ident[:])
+            for i in range(4):
+                c = 4 * hb + i
+                if unit != "d" and i % 2 == 0:
+                    nc.tensor.matmul(
+                        out=rp[:, i * P : (i + 1) * P],
+                        lhsT=r[:, c : c + 1].to_broadcast([P, P]),
+                        rhs=ident[:],
+                        start=True,
+                        stop=True,
+                    )
+                else:
+                    nc.tensor.transpose(rp[:, i * P : (i + 1) * P], r[:, c : c + 1].to_broadcast([P, P]), ident[:])
             rbank[(l, unit, hb)] = rp
 
-        def scale(eng, dst, w, j0, n0, rsrc, q0, nq):
+        def scale_block(eng, dst, w, j0, cb, rsrc):
             eng.tensor_tensor(
-                out=dst.rearrange("p (q e j) -> p q j e", q=nq, e=2, j=4),
-                in0=w[:, j0 : j0 + 4, n0 : n0 + 2 * nq].rearrange("p j (q e) -> p q j e", e=2),
-                in1=rsrc.rearrange("p (e q) -> p q e", e=2)[:, q0 : q0 + nq, :].unsqueeze(2).to_broadcast([P, nq, 4, 2]),
+                out=dst.rearrange("p (w e j) -> p w j e", w=P, e=2, j=4),
+                in0=w[:, j0 : j0 + 4, 256 * cb : 256 * cb + 256].rearrange("p j (w e) -> p w j e", e=2),
+                in1=rsrc.rearrange("p (e w) -> p w e", e=2).unsqueeze(2).to_broadcast([P, P, 4, 2]),
                 op=ALU.mult,
             )
 
@@ -162,23 +168,23 @@ def tile_npertokenswishglu_kernel(tc, x, W_gate, W_up, W_down, s_u, s_v, out):
             t = work.tile([P, 512], F32, tag="rds", name="rds")
             nc.scalar.copy(out=t[:], in_=rbank[(l, "d", 0)][:])
             rsb[l] = t
-
-        def bd_alloc(l):
             gt[(l, "d")] = grp.tile([P, 4 * F], BF16, tag="G", name="dg", align_bytes=64)
 
-        def bd_v(l):
-            scale(nc.vector, gt[(l, "d")][:, 0:1024], wt[(l, "d")], 0, 0, rbank[(l, "d", 0)][:], 0, 128)
-
-        def bd_g(l, c, i):
-            o = c * 2048 + i * 1024
-            scale(nc.gpsimd, gt[(l, "d")][:, o : o + 1024], wt[(l, "d")], 4 * c, 256 * i, rsb[l][:], 128 * i, 128)
+        def bd(l, i):
+            c, cb = i // 2, i % 2
+            eng = nc.gpsimd if BD_ENG[i] == "g" else nc.vector
+            rsrc = rsb[l] if BD_ENG[i] == "g" else rbank[(l, "d", 0)]
+            scale_block(eng, gt[(l, "d")][:, i * 1024 : (i + 1) * 1024], wt[(l, "d")], 4 * c, cb, rsrc[:, 256 * cb : 256 * cb + 256])
 
         def bgu(l, unit, hb):
             if hb == 0:
                 gt[(l, unit)] = grp.tile([P, 4 * F], BF16, tag="G", name="gg", align_bytes=64)
-            scale(
-                nc.vector, gt[(l, unit)][:, hb * 2048 : (hb + 1) * 2048], wt[(l, unit)], 0, 512 * hb, rbank[(l, unit, hb)][:], 0, 256
-            )
+            rp = rbank[(l, unit, hb)]
+            for i in range(2):
+                cb = 2 * hb + i
+                scale_block(
+                    nc.vector, gt[(l, unit)][:, cb * 1024 : (cb + 1) * 1024], wt[(l, unit)], 0, cb, rp[:, 256 * i : 256 * i + 256]
+                )
 
         def cq(l, unit):
             c = code.tile([P, F], U32, tag="c" + unit, name="cw", align_bytes=64)
@@ -214,6 +220,8 @@ def tile_npertokenswishglu_kernel(tc, x, W_gate, W_up, W_down, s_u, s_v, out):
             st[(l, "sil", c)] = sil
 
         def stt(l, c):
+            if c == 0:
+                st[(l, "hg")] = work.tile([P, 2 * B * 4], BF16, tag="hg", name="hg", align_bytes=64)
             hb16 = work.tile([P, 4, B], BF16, tag="hb16", name="hb16")
             ups = st[(l, "ups", c)]
             sil = st[(l, "sil", c)]
@@ -227,18 +235,9 @@ def tile_npertokenswishglu_kernel(tc, x, W_gate, W_up, W_down, s_u, s_v, out):
                     op0=ALU.mult,
                     op1=ALU.mult,
                 )
-            st[(l, "hb16", c)] = hb16
-
-        def rg(l, c):
-            if c == 0:
-                st[(l, "hg")] = work.tile([P, 2 * B * 4], BF16, tag="hg", name="hg", align_bytes=64)
-            nc.gpsimd.tensor_scalar(
+            nc.vector.tensor_copy(
                 out=st[(l, "hg")][:, c * 512 : (c + 1) * 512].rearrange("p (b t) -> p b t", t=4),
-                in0=st[(l, "hb16", c)][:].rearrange("p t b -> p b t"),
-                scalar1=1.0,
-                scalar2=0.0,
-                op0=ALU.mult,
-                op1=ALU.add,
+                in_=hb16[:].rearrange("p t b -> p b t"),
             )
 
         def ch(l):
@@ -278,93 +277,94 @@ def tile_npertokenswishglu_kernel(tc, x, W_gate, W_up, W_down, s_u, s_v, out):
 
         def cp(l):
             ob = work.tile([P, D], F32, tag="ob", name="ob")
-            nc.scalar.activation(out=ob[:], in_=st[(l, "ops")][:], func=ACT.Copy, scale=st[(l, "ro")][:])
+            nc.scalar.activation(
+                out=ob[:],
+                in_=st[(l, "ops")][:],
+                func=ACT.Copy,
+                scale=st[(l, "ro")][:],
+            )
             nc.sync.dma_start(out=out[:, l, :], in_=ob[:])
 
-        def on(l):
-            return 0 <= l < L
+        for unit in ("d", "g", "u"):
+            load(0, unit)
+        load_x()
+        for it in range(L + 2):
+            a, b, m = it, it - 1, it - 2
+            ha, hb_, hm = a < L, 0 <= b < L, 0 <= m < L
 
-        for it in range(-1, L + 3):
-            a, p, q, r = it, it - 1, it - 2, it - 3
-            if on(a + 1):
+            def A(k):
+                if ha:
+                    a_item(a, k)
+
+            if a + 1 < L:
                 for unit in ("d", "g", "u"):
                     load(a + 1, unit)
-                if a + 1 == 0:
-                    load_x()
-            for k in range(12):
-                if k == 0 and on(p):
-                    rc(p)
-                if on(a):
-                    a_s(a, k)
-                nl, nk = (a, k + 2) if k + 2 < 12 else (a + 1, k - 10)
-                if on(nl):
-                    a_t(nl, nk)
-                if k == 0:
-                    if on(p):
-                        bd_alloc(p)
-                        bd_v(p)
-                        bd_g(p, 0, 1)
-                    if on(q):
-                        m1(q, 0)
-                elif k == 1:
-                    if on(p):
-                        bgu(p, "g", 0)
-                        sp(p, "g", 1)
-                        bd_g(p, 1, 0)
-                elif k == 2:
-                    if on(q):
-                        si(q, 0)
-                elif k == 3:
-                    if on(p):
-                        bgu(p, "g", 1)
-                        sp(p, "u", 0)
-                        bd_g(p, 1, 1)
-                elif k == 4:
-                    if on(q):
-                        stt(q, 0)
-                        rg(q, 0)
-                    if on(r):
-                        m2(r)
-                elif k == 5:
-                    if on(p):
-                        bgu(p, "u", 0)
-                    if on(q):
-                        m1(q, 1)
-                    if on(r):
-                        sq(r)
-                elif k == 6:
-                    if on(p):
-                        sp(p, "u", 1)
-                    if on(a):
-                        pw(a, "d")
-                    if on(r):
-                        po(r)
-                elif k == 7:
-                    if on(q):
-                        si(q, 1)
-                elif k == 8:
-                    if on(q):
-                        stt(q, 1)
-                        rg(q, 1)
-                    if on(p):
-                        bgu(p, "u", 1)
-                    if on(r):
-                        cp(r)
-                elif k == 9:
-                    if on(a):
-                        sp(a, "d", 0)
-                        pw(a, "g")
-                elif k == 10:
-                    if on(p):
-                        cq(p, "g")
-                        cq(p, "u")
-                else:
-                    if on(p):
-                        cq(p, "d")
-                    if on(q):
-                        ch(q)
-                    if on(a):
-                        sp(a, "g", 0)
-                        pw(a, "u")
-                    if a == 0:
-                        prep_x()
+            if hm:
+                m1(m, 0)
+            if hb_:
+                rc(b)
+                bd(b, 0)
+                bd(b, 1)
+                bd(b, 2)
+            A(0)
+            A(1)
+            if hb_:
+                bgu(b, "g", 0)
+            if hm:
+                si(m, 0)
+            A(2)
+            if hm:
+                stt(m, 0)
+            A(3)
+            if hb_:
+                sp(b, "g", 1)
+            if ha:
+                pw(a, "d")
+            if hb_:
+                bgu(b, "g", 1)
+            A(4)
+            A(5)
+            if hm:
+                m1(m, 1)
+            if hb_:
+                sp(b, "u", 0)
+            if hm:
+                si(m, 1)
+            if hb_:
+                bd(b, 3)
+                bgu(b, "u", 0)
+            A(6)
+            if hb_:
+                cq(b, "g")
+            A(7)
+            if ha:
+                pw(a, "g")
+            if hm:
+                stt(m, 1)
+                ch(m)
+            if hb_:
+                sp(b, "u", 1)
+            A(8)
+            if hb_:
+                bgu(b, "u", 1)
+            A(9)
+            A(10)
+            if hm:
+                m2(m)
+                sq(m)
+                po(m)
+            if hb_:
+                cq(b, "u")
+            if ha:
+                sp(a, "d", 0)
+            A(11)
+            if ha:
+                pw(a, "u")
+            if hm:
+                cp(m)
+            if hb_:
+                cq(b, "d")
+            if ha:
+                sp(a, "g", 0)
+            if it == 0:
+                prep_x()

@@ -16,8 +16,6 @@ P = 128
 B, L, D, F = 128, 8, 512, 1024
 FLOPS = 2 * B * L * (D * F * 2 + F * D)
 EPS2 = 1e-24
-MANUAL = True
-BD_ENG = ['v','v','g','g']
 
 
 def tile_npertokenswishglu_kernel(tc, x, W_gate, W_up, W_down, s_u, s_v, out):
@@ -32,15 +30,14 @@ def tile_npertokenswishglu_kernel(tc, x, W_gate, W_up, W_down, s_u, s_v, out):
         pt = ctx.enter_context(tc.psum_pool(name="pt", bufs=3))
         pr = ctx.enter_context(tc.psum_pool(name="pr", bufs=2))
         pm = ctx.enter_context(tc.psum_pool(name="pm", bufs=1))
-        if MANUAL:
-            ctx.enter_context(tc.manual_schedule())
+        ctx.enter_context(tc.manual_schedule())
 
         ident = const.tile([P, P], F32)
         make_identity(nc, ident[:])
-        mhalf = const.tile([P, 8], F32)
-        nc.vector.memset(mhalf[:], -0.5)
         identb = const.tile([P, P], BF16)
         make_identity(nc, identb[:])
+        mhalf = const.tile([P, 8], F32)
+        nc.vector.memset(mhalf[:], -0.5)
         gz = const.tile([P, P], BF16)
         nc.vector.memset(gz[:], 0.0)
         xs = const.tile([P, L, D], BF16)
@@ -51,6 +48,7 @@ def tile_npertokenswishglu_kernel(tc, x, W_gate, W_up, W_down, s_u, s_v, out):
         sv = const.tile([P, 8], F32)
 
         wt = {}
+        tbank = {}
         nsq = {}
         rr = {}
         rbank = {}
@@ -62,10 +60,7 @@ def tile_npertokenswishglu_kernel(tc, x, W_gate, W_up, W_down, s_u, s_v, out):
         def load(l, unit):
             if unit == "d":
                 t = wpool.tile([P, 8, D], BF16, tag="W", name="wd")
-                nc.sync.dma_start(
-                    out=t[:],
-                    in_=W_down[l].rearrange("(g p) n -> p g n", g=8, p=P),
-                )
+                nc.sync.dma_start(out=t[:], in_=W_down[l].rearrange("(g p) n -> p g n", g=8, p=P))
             else:
                 W = W_gate if unit == "g" else W_up
                 t = wpool.tile([P, 4, F], BF16, tag="W", name="wg")
@@ -84,7 +79,7 @@ def tile_npertokenswishglu_kernel(tc, x, W_gate, W_up, W_down, s_u, s_v, out):
             xw = xs[:].bitcast(F32)
             xgw = xg[:].bitcast(F32).rearrange("p (l b u) -> p l b u", l=L, b=B, u=2)
             for lp in range(L // 2):
-                xt = pt.tile([P, 512], F32, tag="T", name="xt")
+                xt = pm.tile([P, 512], F32, tag="UV"[lp % 2], name="xt")
                 for i in range(2):
                     for u in range(2):
                         nc.tensor.transpose(
@@ -96,27 +91,33 @@ def tile_npertokenswishglu_kernel(tc, x, W_gate, W_up, W_down, s_u, s_v, out):
                     out=xgw[:, 2 * lp : 2 * lp + 2, :, :],
                     in_=xt[:].rearrange("p (i u b) -> p i b u", i=2, u=2, b=B),
                 )
-            gp = pt.tile([P, 1024], BF16, tag="T", name="gp")
+            gp = pm.tile([P, 1024], BF16, tag="O", name="gp")
             nc.tensor.transpose(gp[:, 0:P], gz[:], identb[:])
             nc.scalar.activation(out=su[:], in_=gp[:, 0:8], func=ACT.Abs)
             nc.scalar.activation(out=sv[:], in_=gp[:, 8:16], func=ACT.Abs, scale=math.sqrt(D))
             nc.vector.quantize_mx(out=xc[:].bitcast(FP8X4), scales=xsc[:], in_=xg[:])
 
-        def a_item(l, k):
+        def which(k):
             if k < 4:
-                unit, cb, hf = "d", k // 2, k % 2
-            elif k < 8:
-                unit, cb, hf = "g", k - 4, 0
-            else:
-                unit, cb, hf = "u", k - 8, 0
-            if k % 4 == 0:
-                shape = [P, 2, 4] if unit == "d" else [P, 1, 8]
-                nsq[(l, unit)] = small.tile(shape, F32, tag="nsq" + unit, name="nsq")
+                return "d", k // 2, k % 2
+            if k < 8:
+                return "g", k - 4, 0
+            return "u", k - 8, 0
+
+        def a_t(l, k):
+            unit, cb, hf = which(k)
             ww = wt[(l, unit)][:].bitcast(F32)
             tp = pt.tile([P, 512], F32, tag="T", name="tp")
             for j in range(4):
                 nc.tensor.transpose(tp[:, j * P : (j + 1) * P], ww[:, 4 * hf + j, cb * P : (cb + 1) * P], ident[:])
-            tv = tp[:].bitcast(BF16).rearrange("p (k e) -> p k e", e=2)
+            tbank[(l, k)] = tp
+
+        def a_s(l, k):
+            unit, cb, hf = which(k)
+            if k % 4 == 0:
+                shape = [P, 2, 4] if unit == "d" else [P, 1, 8]
+                nsq[(l, unit)] = small.tile(shape, F32, tag="nsq" + unit, name="nsq")
+            tv = tbank[(l, k)][:].bitcast(BF16).rearrange("p (k e) -> p k e", e=2)
             for e in range(2):
                 junk = work.tile([P, 512], BF16, tag="junk", name="junk")
                 nc.scalar.activation(
@@ -142,49 +143,42 @@ def tile_npertokenswishglu_kernel(tc, x, W_gate, W_up, W_down, s_u, s_v, out):
         def sp(l, unit, hb):
             r = rr[(l, unit)]
             rp = pr.tile([P, 512], F32, tag="R", name="rp")
-            for i in range(4):
-                c = 4 * hb + i
-                if unit != "d" and i % 2 == 0:
-                    nc.tensor.matmul(
-                        out=rp[:, i * P : (i + 1) * P],
-                        lhsT=r[:, c : c + 1].to_broadcast([P, P]),
-                        rhs=ident[:],
-                        start=True,
-                        stop=True,
-                    )
-                else:
-                    nc.tensor.transpose(rp[:, i * P : (i + 1) * P], r[:, c : c + 1].to_broadcast([P, P]), ident[:])
+            for e in range(2):
+                for i in range(2):
+                    c = 2 * (2 * hb + i) + e
+                    o = (2 * e + i) * P
+                    nc.tensor.transpose(rp[:, o : o + P], r[:, c : c + 1].to_broadcast([P, P]), ident[:])
             rbank[(l, unit, hb)] = rp
 
-        def scale_block(eng, dst, w, j0, cb, rsrc):
+        def scale(eng, dst, w, j0, n0, rsrc, q0, nq):
             eng.tensor_tensor(
-                out=dst.rearrange("p (w e j) -> p w j e", w=P, e=2, j=4),
-                in0=w[:, j0 : j0 + 4, 256 * cb : 256 * cb + 256].rearrange("p j (w e) -> p w j e", e=2),
-                in1=rsrc.rearrange("p (e w) -> p w e", e=2).unsqueeze(2).to_broadcast([P, P, 4, 2]),
+                out=dst.rearrange("p (q e j) -> p q j e", q=nq, e=2, j=4),
+                in0=w[:, j0 : j0 + 4, n0 : n0 + 2 * nq].rearrange("p j (q e) -> p q j e", e=2),
+                in1=rsrc.rearrange("p (e q) -> p q e", e=2)[:, q0 : q0 + nq, :].unsqueeze(2).to_broadcast([P, nq, 4, 2]),
                 op=ALU.mult,
             )
 
         def rc(l):
             t = work.tile([P, 512], F32, tag="rds", name="rds")
-            nc.scalar.copy(out=t[:], in_=rbank[(l, "d", 0)][:])
+            nc.vector.tensor_copy(out=t[:], in_=rbank[(l, "d", 0)][:])
             rsb[l] = t
+
+        def bd_alloc(l):
             gt[(l, "d")] = grp.tile([P, 4 * F], BF16, tag="G", name="dg", align_bytes=64)
 
-        def bd(l, i):
-            c, cb = i // 2, i % 2
-            eng = nc.gpsimd if BD_ENG[i] == "g" else nc.vector
-            rsrc = rsb[l] if BD_ENG[i] == "g" else rbank[(l, "d", 0)]
-            scale_block(eng, gt[(l, "d")][:, i * 1024 : (i + 1) * 1024], wt[(l, "d")], 4 * c, cb, rsrc[:, 256 * cb : 256 * cb + 256])
+        def bd_v(l):
+            scale(nc.vector, gt[(l, "d")][:, 0:2048], wt[(l, "d")], 0, 0, rbank[(l, "d", 0)][:], 0, 256)
+
+        def bd_g(l, c, i):
+            o = c * 2048 + i * 1024
+            scale(nc.gpsimd, gt[(l, "d")][:, o : o + 1024], wt[(l, "d")], 4 * c, 256 * i, rsb[l][:], 128 * i, 128)
 
         def bgu(l, unit, hb):
             if hb == 0:
                 gt[(l, unit)] = grp.tile([P, 4 * F], BF16, tag="G", name="gg", align_bytes=64)
-            rp = rbank[(l, unit, hb)]
-            for i in range(2):
-                cb = 2 * hb + i
-                scale_block(
-                    nc.vector, gt[(l, unit)][:, cb * 1024 : (cb + 1) * 1024], wt[(l, unit)], 0, cb, rp[:, 256 * i : 256 * i + 256]
-                )
+            scale(
+                nc.vector, gt[(l, unit)][:, hb * 2048 : (hb + 1) * 2048], wt[(l, unit)], 0, 512 * hb, rbank[(l, unit, hb)][:], 0, 256
+            )
 
         def cq(l, unit):
             c = code.tile([P, F], U32, tag="c" + unit, name="cw", align_bytes=64)
@@ -220,8 +214,6 @@ def tile_npertokenswishglu_kernel(tc, x, W_gate, W_up, W_down, s_u, s_v, out):
             st[(l, "sil", c)] = sil
 
         def stt(l, c):
-            if c == 0:
-                st[(l, "hg")] = work.tile([P, 2 * B * 4], BF16, tag="hg", name="hg", align_bytes=64)
             hb16 = work.tile([P, 4, B], BF16, tag="hb16", name="hb16")
             ups = st[(l, "ups", c)]
             sil = st[(l, "sil", c)]
@@ -235,9 +227,18 @@ def tile_npertokenswishglu_kernel(tc, x, W_gate, W_up, W_down, s_u, s_v, out):
                     op0=ALU.mult,
                     op1=ALU.mult,
                 )
-            nc.vector.tensor_copy(
+            st[(l, "hb16", c)] = hb16
+
+        def rg(l, c):
+            if c == 0:
+                st[(l, "hg")] = work.tile([P, 2 * B * 4], BF16, tag="hg", name="hg", align_bytes=64)
+            nc.gpsimd.tensor_scalar(
                 out=st[(l, "hg")][:, c * 512 : (c + 1) * 512].rearrange("p (b t) -> p b t", t=4),
-                in_=hb16[:].rearrange("p t b -> p b t"),
+                in0=st[(l, "hb16", c)][:].rearrange("p t b -> p b t"),
+                scalar1=1.0,
+                scalar2=0.0,
+                op0=ALU.mult,
+                op1=ALU.add,
             )
 
         def ch(l):
@@ -277,94 +278,92 @@ def tile_npertokenswishglu_kernel(tc, x, W_gate, W_up, W_down, s_u, s_v, out):
 
         def cp(l):
             ob = work.tile([P, D], F32, tag="ob", name="ob")
-            nc.scalar.activation(
-                out=ob[:],
-                in_=st[(l, "ops")][:],
-                func=ACT.Copy,
-                scale=st[(l, "ro")][:],
-            )
+            nc.vector.tensor_scalar_mul(out=ob[:], in0=st[(l, "ops")][:], scalar1=st[(l, "ro")][:])
             nc.sync.dma_start(out=out[:, l, :], in_=ob[:])
 
-        for unit in ("d", "g", "u"):
-            load(0, unit)
-        load_x()
-        for it in range(L + 2):
-            a, b, m = it, it - 1, it - 2
-            ha, hb_, hm = a < L, 0 <= b < L, 0 <= m < L
+        def on(l):
+            return 0 <= l < L
 
-            def A(k):
-                if ha:
-                    a_item(a, k)
-
-            if a + 1 < L:
+        for it in range(-1, L + 3):
+            a, p, q, r = it, it - 1, it - 2, it - 3
+            if on(a + 1):
                 for unit in ("d", "g", "u"):
                     load(a + 1, unit)
-            if hm:
-                m1(m, 0)
-            if hb_:
-                rc(b)
-                bd(b, 0)
-                bd(b, 1)
-                bd(b, 2)
-            A(0)
-            A(1)
-            if hb_:
-                bgu(b, "g", 0)
-            if hm:
-                si(m, 0)
-            A(2)
-            if hm:
-                stt(m, 0)
-            A(3)
-            if hb_:
-                sp(b, "g", 1)
-            if ha:
-                pw(a, "d")
-            if hb_:
-                bgu(b, "g", 1)
-            A(4)
-            A(5)
-            if hm:
-                m1(m, 1)
-            if hb_:
-                sp(b, "u", 0)
-            if hm:
-                si(m, 1)
-            if hb_:
-                bd(b, 3)
-                bgu(b, "u", 0)
-            A(6)
-            if hb_:
-                cq(b, "g")
-            A(7)
-            if ha:
-                pw(a, "g")
-            if hm:
-                stt(m, 1)
-                ch(m)
-            if hb_:
-                sp(b, "u", 1)
-            A(8)
-            if hb_:
-                bgu(b, "u", 1)
-            A(9)
-            A(10)
-            if hm:
-                m2(m)
-                sq(m)
-                po(m)
-            if hb_:
-                cq(b, "u")
-            if ha:
-                sp(a, "d", 0)
-            A(11)
-            if ha:
-                pw(a, "u")
-            if hm:
-                cp(m)
-            if hb_:
-                cq(b, "d")
-            if ha:
-                sp(a, "g", 0)
-            if it == 0:
-                prep_x()
+                if a + 1 == 0:
+                    load_x()
+            for k in range(12):
+                if k == 0 and on(p):
+                    rc(p)
+                if on(a):
+                    a_s(a, k)
+                nl, nk = (a, k + 2) if k + 2 < 12 else (a + 1, k - 10)
+                if on(nl):
+                    a_t(nl, nk)
+                if k == 0:
+                    if on(p):
+                        bd_alloc(p)
+                        bd_v(p)
+                        bd_g(p, 1, 0)
+                    if on(q):
+                        m1(q, 0)
+                elif k == 1:
+                    if on(p):
+                        bgu(p, "g", 0)
+                        sp(p, "g", 1)
+                        bd_g(p, 1, 1)
+                elif k == 2:
+                    if on(q):
+                        si(q, 0)
+                elif k == 3:
+                    if on(p):
+                        bgu(p, "g", 1)
+                        sp(p, "u", 0)
+                elif k == 4:
+                    if on(q):
+                        stt(q, 0)
+                        rg(q, 0)
+                    if on(r):
+                        m2(r)
+                elif k == 5:
+                    if on(p):
+                        bgu(p, "u", 0)
+                    if on(q):
+                        m1(q, 1)
+                    if on(r):
+                        sq(r)
+                elif k == 6:
+                    if on(p):
+                        sp(p, "u", 1)
+                    if on(a):
+                        pw(a, "d")
+                    if on(r):
+                        po(r)
+                elif k == 7:
+                    if on(q):
+                        si(q, 1)
+                elif k == 8:
+                    if on(q):
+                        stt(q, 1)
+                        rg(q, 1)
+                    if on(p):
+                        bgu(p, "u", 1)
+                    if on(r):
+                        cp(r)
+                elif k == 9:
+                    if on(a):
+                        sp(a, "d", 0)
+                        pw(a, "g")
+                elif k == 10:
+                    if on(p):
+                        cq(p, "g")
+                        cq(p, "u")
+                else:
+                    if on(p):
+                        cq(p, "d")
+                    if on(q):
+                        ch(q)
+                    if on(a):
+                        sp(a, "g", 0)
+                        pw(a, "u")
+                    if a == 0:
+                        prep_x()

import math
from contextlib import ExitStack

from concourse import mybir
from concourse.masks import make_identity

F32 = mybir.dt.float32
BF16 = mybir.dt.bfloat16
U32 = mybir.dt.uint32
U8 = mybir.dt.uint8
FP8X4 = mybir.dt.float8_e4m3fn_x4
ACT = mybir.ActivationFunctionType
ALU = mybir.AluOpType

P = 128
B, L, D, F = 128, 8, 512, 1024
FLOPS = 2 * B * L * (D * F * 2 + F * D)
EPS2 = 1e-24


def tile_npertokenswishglu_kernel(tc, x, W_gate, W_up, W_down, s_u, s_v, out):
    nc = tc.nc
    with ExitStack() as ctx:
        const = ctx.enter_context(tc.tile_pool(name="const", bufs=1))
        wpool = ctx.enter_context(tc.tile_pool(name="wpool", bufs=9))
        grp = ctx.enter_context(tc.tile_pool(name="grp", bufs=4))
        code = ctx.enter_context(tc.tile_pool(name="code", bufs=2))
        small = ctx.enter_context(tc.tile_pool(name="small", bufs=3))
        work = ctx.enter_context(tc.tile_pool(name="work", bufs=2))
        pt = ctx.enter_context(tc.psum_pool(name="pt", bufs=3))
        pr = ctx.enter_context(tc.psum_pool(name="pr", bufs=2))
        pm = ctx.enter_context(tc.psum_pool(name="pm", bufs=1))
        ctx.enter_context(tc.manual_schedule())

        ident = const.tile([P, P], F32)
        make_identity(nc, ident[:])
        identb = const.tile([P, P], BF16)
        make_identity(nc, identb[:])
        mhalf = const.tile([P, 8], F32)
        nc.vector.memset(mhalf[:], -0.5)
        gz = const.tile([P, P], BF16)
        nc.vector.memset(gz[:], 0.0)
        xs = const.tile([P, L, D], BF16)
        xg = const.tile([P, L * B * 4], BF16, align_bytes=64)
        xc = const.tile([P, L * B], U32, align_bytes=64)
        xsc = const.tile([P, L * B], U8, align_bytes=64)
        su = const.tile([P, 8], F32)
        sv = const.tile([P, 8], F32)

        wt = {}
        tbank = {}
        nsq = {}
        rr = {}
        rbank = {}
        rsb = {}
        gt = {}
        cod = {}
        st = {}

        def load(l, unit):
            if unit == "d":
                t = wpool.tile([P, 8, D], BF16, tag="W", name="wd")
                nc.sync.dma_start(out=t[:], in_=W_down[l].rearrange("(g p) n -> p g n", g=8, p=P))
            else:
                W = W_gate if unit == "g" else W_up
                t = wpool.tile([P, 4, F], BF16, tag="W", name="wg")
                nc.sync.dma_start(
                    out=t[:].rearrange("p (u e) n -> p u (e n)", u=2),
                    in_=W[l].rearrange("(u p e) n -> p u (e n)", u=2, p=P, e=2),
                )
            wt[(l, unit)] = t

        def load_x():
            nc.sync.dma_start(out=xs[:], in_=x)
            nc.sync.dma_start(out=gz[0:8, :], in_=s_u.rearrange("o (t p) -> (o t) p", t=8))
            nc.sync.dma_start(out=gz[8:16, :], in_=s_v.rearrange("o (t p) -> (o t) p", t=8))

        def prep_x():
            xw = xs[:].bitcast(F32)
            xgw = xg[:].bitcast(F32).rearrange("p (l b u) -> p l b u", l=L, b=B, u=2)
            for lp in range(L // 2):
                xt = pm.tile([P, 512], F32, tag="UV"[lp % 2], name="xt")
                for i in range(2):
                    for u in range(2):
                        nc.tensor.transpose(
                            xt[:, (2 * i + u) * P : (2 * i + u + 1) * P],
                            xw[:, 2 * lp + i, u * P : (u + 1) * P],
                            ident[:],
                        )
                nc.vector.tensor_copy(
                    out=xgw[:, 2 * lp : 2 * lp + 2, :, :],
                    in_=xt[:].rearrange("p (i u b) -> p i b u", i=2, u=2, b=B),
                )
            gp = pm.tile([P, 1024], BF16, tag="O", name="gp")
            nc.tensor.transpose(gp[:, 0:P], gz[:], identb[:])
            nc.scalar.activation(out=su[:], in_=gp[:, 0:8], func=ACT.Abs)
            nc.scalar.activation(out=sv[:], in_=gp[:, 8:16], func=ACT.Abs, scale=math.sqrt(D))
            nc.vector.quantize_mx(out=xc[:].bitcast(FP8X4), scales=xsc[:], in_=xg[:])

        def which(k):
            if k < 4:
                return "d", k // 2, k % 2
            if k < 8:
                return "g", k - 4, 0
            return "u", k - 8, 0

        def a_t(l, k):
            unit, cb, hf = which(k)
            ww = wt[(l, unit)][:].bitcast(F32)
            tp = pt.tile([P, 512], F32, tag="T", name="tp")
            for j in range(4):
                nc.tensor.transpose(tp[:, j * P : (j + 1) * P], ww[:, 4 * hf + j, cb * P : (cb + 1) * P], ident[:])
            tbank[(l, k)] = tp

        def a_s(l, k):
            unit, cb, hf = which(k)
            if k % 4 == 0:
                shape = [P, 2, 4] if unit == "d" else [P, 1, 8]
                nsq[(l, unit)] = small.tile(shape, F32, tag="nsq" + unit, name="nsq")
            tv = tbank[(l, k)][:].bitcast(BF16).rearrange("p (k e) -> p k e", e=2)
            for e in range(2):
                junk = work.tile([P, 512], BF16, tag="junk", name="junk")
                nc.scalar.activation(
                    out=junk[:],
                    in_=tv[:, :, e],
                    func=ACT.Square,
                    accum_out=nsq[(l, unit)][:, hf, 2 * cb + e : 2 * cb + e + 1],
                )

        def pw(l, unit):
            n = 4 if unit == "d" else 8
            q = nsq[(l, unit)]
            xx = small.tile([P, n], F32, tag="xx" + unit, name="xx")
            if unit == "d":
                nc.gpsimd.tensor_tensor(out=xx[:], in0=q[:, 0, :], in1=q[:, 1, :], op=ALU.add)
                nc.gpsimd.tensor_scalar_max(out=xx[:], in0=xx[:], scalar1=EPS2)
            else:
                nc.gpsimd.tensor_scalar_max(out=xx[:], in0=q[:, 0, :], scalar1=EPS2)
            r = small.tile([P, n], F32, tag="r" + unit, name="r")
            nc.gpsimd.tensor_tensor(out=r[:], in0=xx[:], in1=mhalf[:, 0:n], op=ALU.pow)
            rr[(l, unit)] = r

        def sp(l, unit, hb):
            r = rr[(l, unit)]
            rp = pr.tile([P, 512], F32, tag="R", name="rp")
            for e in range(2):
                for i in range(2):
                    c = 2 * (2 * hb + i) + e
                    o = (2 * e + i) * P
                    nc.tensor.transpose(rp[:, o : o + P], r[:, c : c + 1].to_broadcast([P, P]), ident[:])
            rbank[(l, unit, hb)] = rp

        def scale(eng, dst, w, j0, n0, rsrc, q0, nq):
            eng.tensor_tensor(
                out=dst.rearrange("p (q e j) -> p q j e", q=nq, e=2, j=4),
                in0=w[:, j0 : j0 + 4, n0 : n0 + 2 * nq].rearrange("p j (q e) -> p q j e", e=2),
                in1=rsrc.rearrange("p (e q) -> p q e", e=2)[:, q0 : q0 + nq, :].unsqueeze(2).to_broadcast([P, nq, 4, 2]),
                op=ALU.mult,
            )

        def rc(l):
            t = work.tile([P, 512], F32, tag="rds", name="rds")
            nc.vector.tensor_copy(out=t[:], in_=rbank[(l, "d", 0)][:])
            rsb[l] = t

        def bd_alloc(l):
            gt[(l, "d")] = grp.tile([P, 4 * F], BF16, tag="G", name="dg", align_bytes=64)

        def bd_v(l):
            scale(nc.vector, gt[(l, "d")][:, 0:2048], wt[(l, "d")], 0, 0, rbank[(l, "d", 0)][:], 0, 256)

        def bd_g(l, c, i):
            o = c * 2048 + i * 1024
            scale(nc.gpsimd, gt[(l, "d")][:, o : o + 1024], wt[(l, "d")], 4 * c, 256 * i, rsb[l][:], 128 * i, 128)

        def bgu(l, unit, hb):
            if hb == 0:
                gt[(l, unit)] = grp.tile([P, 4 * F], BF16, tag="G", name="gg", align_bytes=64)
            scale(
                nc.vector, gt[(l, unit)][:, hb * 2048 : (hb + 1) * 2048], wt[(l, unit)], 0, 512 * hb, rbank[(l, unit, hb)][:], 0, 256
            )

        def cq(l, unit):
            c = code.tile([P, F], U32, tag="c" + unit, name="cw", align_bytes=64)
            s = code.tile([P, F], U8, tag="s" + unit, name="cs", align_bytes=64)
            nc.vector.quantize_mx(out=c[:].bitcast(FP8X4), scales=s[:], in_=gt[(l, unit)][:])
            cod[(l, unit)] = (c, s)

        def m1(l, c):
            ups = pm.tile([P, 512], F32, tag="U", name="ups")
            vps = pm.tile([P, 512], F32, tag="V", name="vps")
            for dstp, unit in ((vps, "u"), (ups, "g")):
                cc, ss = cod[(l, unit)]
                for i in range(4):
                    t = 4 * c + i
                    nc.tensor.matmul_mx(
                        out=dstp[:, i * P : (i + 1) * P],
                        lhsT=cc[:, t * P : (t + 1) * P].bitcast(FP8X4),
                        lhsT_scale=ss[:, t * P : (t + 1) * P],
                        rhs=xc[:, l * B : (l + 1) * B].bitcast(FP8X4),
                        rhs_scale=xsc[:, l * B : (l + 1) * B],
                        start=True,
                        stop=True,
                    )
            st[(l, "ups", c)] = ups
            st[(l, "vps", c)] = vps

        def si(l, c):
            sil = work.tile([P, 4, B], F32, tag="sil", name="sil")
            vps = st[(l, "vps", c)]
            for i in range(4):
                t = 4 * c + i
                nc.scalar.activation(out=sil[:, i, :], in_=vps[:, i * P : (i + 1) * P], func=ACT.Silu, scale=sv[:, t : t + 1])
            st[(l, "sil", c)] = sil

        def stt(l, c):
            hb16 = work.tile([P, 4, B], BF16, tag="hb16", name="hb16")
            ups = st[(l, "ups", c)]
            sil = st[(l, "sil", c)]
            for i in range(4):
                t = 4 * c + i
                nc.vector.scalar_tensor_tensor(
                    out=hb16[:, i, :],
                    in0=ups[:, i * P : (i + 1) * P],
                    scalar=su[:, t : t + 1],
                    in1=sil[:, i, :],
                    op0=ALU.mult,
                    op1=ALU.mult,
                )
            st[(l, "hb16", c)] = hb16

        def rg(l, c):
            if c == 0:
                st[(l, "hg")] = work.tile([P, 2 * B * 4], BF16, tag="hg", name="hg", align_bytes=64)
            nc.gpsimd.tensor_scalar(
                out=st[(l, "hg")][:, c * 512 : (c + 1) * 512].rearrange("p (b t) -> p b t", t=4),
                in0=st[(l, "hb16", c)][:].rearrange("p t b -> p b t"),
                scalar1=1.0,
                scalar2=0.0,
                op0=ALU.mult,
                op1=ALU.add,
            )

        def ch(l):
            hc = work.tile([P, 2 * B], U32, tag="hc", name="hc", align_bytes=64)
            hs = work.tile([P, 2 * B], U8, tag="hs", name="hs", align_bytes=64)
            nc.vector.quantize_mx(out=hc[:].bitcast(FP8X4), scales=hs[:], in_=st[(l, "hg")][:])
            st[(l, "hc")] = (hc, hs)

        def m2(l):
            ops = pm.tile([P, 512], F32, tag="O", name="ops")
            hc, hs = st[(l, "hc")]
            dc, ds = cod[(l, "d")]
            for c in range(2):
                nc.tensor.matmul_mx(
                    out=ops[:],
                    lhsT=hc[:, c * B : (c + 1) * B].bitcast(FP8X4),
                    lhsT_scale=hs[:, c * B : (c + 1) * B],
                    rhs=dc[:, c * D : (c + 1) * D].bitcast(FP8X4),
                    rhs_scale=ds[:, c * D : (c + 1) * D],
                    start=(c == 0),
                    stop=(c == 1),
                )
            st[(l, "ops")] = ops

        def sq(l):
            nso = small.tile([P, 1], F32, tag="nso", name="nso")
            junk = work.tile([P, 512], BF16, tag="junk", name="junk")
            nc.scalar.activation(out=junk[:], in_=st[(l, "ops")][:], func=ACT.Square, accum_out=nso[:])
            st[(l, "nso")] = nso

        def po(l):
            nsx = small.tile([P, 1], F32, tag="nsx", name="nsx")
            nc.gpsimd.tensor_scalar_max(out=nsx[:], in0=st[(l, "nso")][:], scalar1=EPS2)
            ro = small.tile([P, 1], F32, tag="ro", name="ro")
            nc.gpsimd.tensor_tensor(out=ro[:], in0=nsx[:], in1=mhalf[:, 0:1], op=ALU.pow)
            st[(l, "ro")] = ro

        def cp(l):
            ob = work.tile([P, D], F32, tag="ob", name="ob")
            nc.vector.tensor_scalar_mul(out=ob[:], in0=st[(l, "ops")][:], scalar1=st[(l, "ro")][:])
            nc.sync.dma_start(out=out[:, l, :], in_=ob[:])

        def on(l):
            return 0 <= l < L

        for it in range(-1, L + 3):
            a, p, q, r = it, it - 1, it - 2, it - 3
            if on(a + 1):
                for unit in ("d", "g", "u"):
                    load(a + 1, unit)
                if a + 1 == 0:
                    load_x()
            for k in range(12):
                if k == 0 and on(p):
                    rc(p)
                if on(a):
                    a_s(a, k)
                nl, nk = (a, k + 2) if k + 2 < 12 else (a + 1, k - 10)
                if on(nl):
                    a_t(nl, nk)
                if k == 0:
                    if on(p):
                        bd_alloc(p)
                        bd_v(p)
                        bd_g(p, 1, 0)
                    if on(q):
                        m1(q, 0)
                elif k == 1:
                    if on(p):
                        bgu(p, "g", 0)
                        sp(p, "g", 1)
                        bd_g(p, 1, 1)
                elif k == 2:
                    if on(q):
                        si(q, 0)
                elif k == 3:
                    if on(p):
                        bgu(p, "g", 1)
                        sp(p, "u", 0)
                elif k == 4:
                    if on(q):
                        stt(q, 0)
                        rg(q, 0)
                    if on(r):
                        m2(r)
                elif k == 5:
                    if on(p):
                        bgu(p, "u", 0)
                    if on(q):
                        m1(q, 1)
                    if on(r):
                        sq(r)
                elif k == 6:
                    if on(p):
                        sp(p, "u", 1)
                    if on(a):
                        pw(a, "d")
                    if on(r):
                        po(r)
                elif k == 7:
                    if on(q):
                        si(q, 1)
                elif k == 8:
                    if on(q):
                        stt(q, 1)
                        rg(q, 1)
                    if on(p):
                        bgu(p, "u", 1)
                    if on(r):
                        cp(r)
                elif k == 9:
                    if on(a):
                        sp(a, "d", 0)
                        pw(a, "g")
                elif k == 10:
                    if on(p):
                        cq(p, "g")
                        cq(p, "u")
                else:
                    if on(p):
                        cq(p, "d")
                    if on(q):
                        ch(q)
                    if on(a):
                        sp(a, "g", 0)
                        pw(a, "u")
                    if a == 0:
                        prep_x()
